import numpy as np
import ml_dtypes


def mxq(x, axis, fmt="e4m3"):
    dtype, down = {"e4m3": (ml_dtypes.float8_e4m3fn, 7), "e5m2": (ml_dtypes.float8_e5m2, 14)}[fmt]
    v = np.moveaxis(np.asarray(x, np.float32).astype(ml_dtypes.bfloat16).astype(np.float64), axis, -1)
    blocks = v.reshape(v.shape[:-1] + (-1, 32))
    amax = np.abs(blocks).max(-1, keepdims=True)
    byte = np.maximum(np.where(amax > 0, np.frexp(amax)[1] - 1 + 127, 0) - down, 1)
    scale = np.exp2(byte - 127.0)
    codes = (blocks / scale).astype(np.float32).astype(dtype).astype(np.float64)
    return np.moveaxis((codes * scale).reshape(v.shape), -1, axis)


WIDE = False


def mx_kscale(k):
    if not WIDE:
        return np.ones(k)
    levels = np.array([10, -10, 5, -5, 0])
    if k % 512:
        return np.exp2(np.random.permutation(np.resize(levels, k // 32))).repeat(32)
    a = np.empty((k // 512, 16))
    for p in range(k // 512):
        a[p, :8] = np.random.permutation(np.resize(levels, 8))
        for g in range(8):
            far = levels[np.abs(levels - a[p, g]) >= 10]
            a[p, g + 8] = far[np.random.randint(len(far))]
    return np.exp2(a.ravel()).repeat(32)


BF16 = ml_dtypes.bfloat16


def bf(x):
    return np.asarray(x, np.float32).astype(BF16)


def f64(x):
    return np.asarray(x).astype(np.float64)


B, S, D, K = 128, 8, 1024, 2048


def setup_inputs():
    t = np.exp2(np.round(np.log2(mx_kscale(D)) / 2))
    q = np.random.standard_normal((B, S, D))
    a = 0.3 * np.random.standard_normal((B, S, 1))
    p = np.random.standard_normal((B, S, D)) + a * q[:, -1:, :]
    W = np.random.uniform(0.0, 1.0, (K, D)) * np.sqrt(12.0 / D)
    return {"p": bf(p / t), "q": bf(q / t), "W": bf(W * t)}


def reference(p, q, W):
    p, q, W = f64(p), f64(q), f64(W)
    W2 = mxq(W * W, 1, "e4m3")
    q_last = q[:, -1, :]
    dot = (mxq(p * q_last[:, None, :], 2, "e4m3") @ W2.T).transpose(0, 2, 1)
    norm_p = np.sqrt((mxq(p * p, 2, "e4m3") @ W2.T).transpose(0, 2, 1))
    norm_q = np.sqrt(mxq(q_last * q_last, 1, "e4m3") @ W2.T)
    dist = -dot / (norm_p * norm_q[:, :, None] * D)
    return dist.reshape(B, S, -1)

@@ -1,0 +1,288 @@
+from contextlib import ExitStack
+
+import concourse.mybir as mybir
+from concourse.masks import make_identity
+
+F32 = mybir.dt.float32
+BF16 = mybir.dt.bfloat16
+U32 = mybir.dt.uint32
+U8 = mybir.dt.uint8
+FP8X4 = mybir.dt.float8_e4m3fn_x4
+ACT = mybir.ActivationFunctionType
+ALU = mybir.AluOpType
+
+P = 128
+B, S, D, K = 128, 8, 1024, 2048
+PASSES = D // (4 * P)
+K_CHUNK = 256
+CHUNKS = K // K_CHUNK
+PAIRS = S // 2
+UNITS = CHUNKS * PAIRS
+AHEAD = 2
+SQUARE_ON_SCALAR = (False, True, True, False)
+NORMS_AHEAD = False
+
+FLOPS = 2 * (2 * B * S + B) * K * D
+
+
+def tile_mpl_kernel(tc, p, q, W, out):
+    nc = tc.nc
+    out_rows = out.rearrange("b s k -> b (s k)")
+    with ExitStack() as ctx:
+        inputs = ctx.enter_context(tc.tile_pool(name="inputs", bufs=1))
+        operands = ctx.enter_context(tc.tile_pool(name="operands", bufs=1))
+        staging = ctx.enter_context(tc.tile_pool(name="staging", bufs=2))
+        results = ctx.enter_context(tc.tile_pool(name="results", bufs=3))
+        banks = ctx.enter_context(tc.psum_pool(name="banks", bufs=8))
+
+        q_rows = inputs.tile([P, D], BF16, name="q_rows")
+        p_rows = [inputs.tile([P, 2, D], BF16, name="p_rows%d" % pair) for pair in range(PAIRS)]
+        w_rows = [inputs.tile([P, 2, D], BF16, name="w_rows%d" % c) for c in range(CHUNKS)]
+
+        def load_p(pair):
+            nc.sync.dma_start(out=p_rows[pair][:], in_=p[:, 2 * pair : 2 * pair + 2, :])
+
+        def load_w(c):
+            rows = W[K_CHUNK * c : K_CHUNK * (c + 1), :]
+            nc.sync.dma_start(out=w_rows[c][:], in_=rows.rearrange("(t r) d -> r t d", r=P))
+
+        load_w(0)
+        load_p(0)
+        nc.sync.dma_start(out=q_rows[:], in_=q[:, S - 1, :])
+        for pair in range(1, PAIRS):
+            load_p(pair)
+        for c in range(1, CHUNKS):
+            load_w(c)
+
+        identity = inputs.tile([P, P], F32, name="identity")
+        make_identity(nc, identity[:])
+        one = inputs.tile([P, 1], F32, name="one")
+        nc.vector.memset(one[:], 1.0)
+        warm = inputs.tile([P, 1], F32, name="warm")
+        nc.scalar.activation(out=warm[:], in_=one[:], func=ACT.Abs_reciprocal_sqrt)
+
+        q_flipped = inputs.tile([P, PASSES, 4 * P], BF16, name="q_flipped")
+        qq_values = inputs.tile([P, PASSES * 4 * P], BF16, name="qq_values", align_bytes=64)
+        qq_codes = operands.tile([P, PASSES * P], U32, name="qq_codes", align_bytes=64)
+        qq_scales = operands.tile([P, PASSES * P], U8, name="qq_scales", align_bytes=64)
+        pq_codes = [operands.tile([P, 512], U32, name="pq_codes%d" % i, align_bytes=64) for i in range(PAIRS)]
+        pq_scales = [operands.tile([P, 512], U8, name="pq_scales%d" % i, align_bytes=64) for i in range(PAIRS)]
+        pp_codes = [operands.tile([P, 512], U32, name="pp_codes%d" % i, align_bytes=64) for i in range(PAIRS)]
+        pp_scales = [operands.tile([P, 512], U8, name="pp_scales%d" % i, align_bytes=64) for i in range(PAIRS)]
+        w2_codes = [operands.tile([P, 512], U32, name="w2_codes%d" % c, align_bytes=64) for c in range(CHUNKS)]
+        w2_scales = [operands.tile([P, 512], U8, name="w2_scales%d" % c, align_bytes=64) for c in range(CHUNKS)]
+        q_factor = [operands.tile([P, K_CHUNK], F32, name="q_factor%d" % c) for c in range(CHUNKS)]
+        live = {}
+
+        def flip(rows, g):
+            bank = banks.tile([P, 512], F32, name="bank")
+            for u in range(2):
+                for t in range(2):
+                    nc.tensor.transpose(
+                        out=bank[:, u * 256 + t * P : u * 256 + (t + 1) * P],
+                        in_=rows[:, t, :].bitcast(F32)[:, 256 * g + u : 256 * (g + 1) : 2],
+                        identity=identity[:],
+                    )
+            return bank
+
+        def copy_words(dst, bank):
+            nc.scalar.copy(
+                out=dst.bitcast(F32).rearrange("p (n u) -> p n u", u=2),
+                in_=bank[:].rearrange("p (u n) -> p n u", u=2),
+            )
+
+        def square_words(dst, bank):
+            nc.scalar.activation(
+                out=dst.rearrange("p (n u e) -> p n u e", u=2, e=2),
+                in_=bank[:].bitcast(BF16).rearrange("p (u n e) -> p n u e", u=2, e=2),
+                func=ACT.Square,
+            )
+
+        def quantise(codes, scales, values):
+            nc.vector.quantize_mx(out=codes[:].bitcast(FP8X4), scales=scales[:], in_=values)
+
+        def q_flip():
+            bank = banks.tile([P, 512], F32, name="bank")
+            for u in range(2):
+                for g in range(PASSES):
+                    nc.tensor.transpose(
+                        out=bank[:, u * 256 + g * P : u * 256 + (g + 1) * P],
+                        in_=q_rows[:].bitcast(F32)[:, 256 * g + u : 256 * (g + 1) : 2],
+                        identity=identity[:],
+                    )
+            live["q"] = bank
+
+        def p_flip(pair):
+            for g in range(PASSES):
+                live["p", pair, g] = flip(p_rows[pair], g)
+
+        def p_copy(pair):
+            if SQUARE_ON_SCALAR[pair]:
+                return
+            flipped = staging.tile([P, PASSES, 1024], BF16, name="p_flipped")
+            live["p_flipped", pair] = flipped
+            for g in range(PASSES):
+                copy_words(flipped[:, g, :], live["p", pair, g])
+
+        def p_square(pair):
+            values = staging.tile([P, PASSES * 1024], BF16, name="pp_values", align_bytes=64)
+            if SQUARE_ON_SCALAR[pair]:
+                for g in range(PASSES):
+                    square_words(values[:, g * 1024 : (g + 1) * 1024], live["p", pair, g])
+            else:
+                flat = live["p_flipped", pair][:].rearrange("p g n -> p (g n)")
+                nc.vector.tensor_tensor(out=values[:], in0=flat, in1=flat, op=ALU.mult)
+            quantise(pp_codes[pair], pp_scales[pair], values[:])
+
+        def p_times_q(pair):
+            values = staging.tile([P, PASSES, 1024], BF16, name="pq_values", align_bytes=64)
+            for g in range(PASSES):
+                if SQUARE_ON_SCALAR[pair]:
+                    nc.vector.tensor_tensor(
+                        out=values[:, g, :].rearrange("p (s n u e) -> p s n u e", s=2, u=2, e=2),
+                        in0=live["p", pair, g][:].bitcast(BF16).rearrange("p (u s n e) -> p s n u e", u=2, s=2, e=2),
+                        in1=q_flipped[:, g, :]
+                        .rearrange("p (n u e) -> p n u e", u=2, e=2)
+                        .unsqueeze(1)
+                        .to_broadcast([P, 2, P, 2, 2]),
+                        op=ALU.mult,
+                    )
+                else:
+                    nc.vector.tensor_tensor(
+                        out=values[:, g, :].rearrange("p (s n) -> p s n", s=2),
+                        in0=live["p_flipped", pair][:, g, :].rearrange("p (s n) -> p s n", s=2),
+                        in1=q_flipped[:, g, :].unsqueeze(1).to_broadcast([P, 2, 4 * P]),
+                        op=ALU.mult,
+                    )
+            quantise(pq_codes[pair], pq_scales[pair], values[:].rearrange("p g n -> p (g n)"))
+
+        def w_flip(c):
+            for g in range(PASSES):
+                live["w", c, g] = flip(w_rows[c], g)
+
+        def w_square(c, g):
+            if g == 0:
+                live["w2", c] = staging.tile([P, PASSES, 1024], BF16, name="w2_values", align_bytes=64)
+            values = live["w2", c]
+            if c == 0:
+                flipped = staging.tile([P, 1024], BF16, name="w_flipped")
+                copy_words(flipped[:], live["w", c, g])
+                nc.vector.tensor_tensor(out=values[:, g, :], in0=flipped[:], in1=flipped[:], op=ALU.mult)
+            else:
+                square_words(values[:, g, :], live["w", c, g])
+
+        def w_quantise(c):
+            quantise(w2_codes[c], w2_scales[c], live["w2", c][:].rearrange("p g n -> p (g n)"))
+
+        def contract(sums, codes, scales, first, step, c):
+            for g in range(PASSES):
+                cols = slice((first + step * g) * P, (first + step * g + 1) * P)
+                k_cols = slice(g * K_CHUNK, (g + 1) * K_CHUNK)
+                nc.tensor.matmul_mx(
+                    out=sums,
+                    lhsT=codes[:, cols].bitcast(FP8X4),
+                    lhsT_scale=scales[:, cols],
+                    rhs=w2_codes[c][:, k_cols].bitcast(FP8X4),
+                    rhs_scale=w2_scales[c][:, k_cols],
+                    start=(g == 0),
+                    stop=(g == PASSES - 1),
+                )
+
+        def q_norm(c):
+            bank = banks.tile([P, 512], F32, name="bank")
+            contract(bank[:, 0:K_CHUNK], qq_codes, qq_scales, 0, 1, c)
+            nc.scalar.activation(
+                out=q_factor[c][:], in_=bank[:, 0:K_CHUNK], func=ACT.Abs_reciprocal_sqrt, scale=float(D * D)
+            )
+
+        def p_norms(unit):
+            c, pair = divmod(unit, PAIRS)
+            bank = banks.tile([P, 512], F32, name="bank")
+            for s in range(2):
+                contract(bank[:, s * K_CHUNK : (s + 1) * K_CHUNK], pp_codes[pair], pp_scales[pair], s, 2, c)
+            factor = results.tile([P, 2 * K_CHUNK], F32, name="p_factor")
+            live["p_factor", unit] = factor
+            nc.scalar.activation(
+                out=factor[:].rearrange("p (k s) -> p k s", s=2),
+                in_=bank[:].rearrange("p (s k) -> p k s", s=2),
+                func=ACT.Abs_reciprocal_sqrt,
+            )
+
+        def dots(unit):
+            c, pair = divmod(unit, PAIRS)
+            bank = banks.tile([P, 512], F32, name="bank")
+            for s in range(2):
+                contract(bank[:, s * K_CHUNK : (s + 1) * K_CHUNK], pq_codes[pair], pq_scales[pair], s, 2, c)
+            if pair == 0:
+                live["cosines", c] = results.tile([P, PAIRS, 2 * K_CHUNK], F32, name="cosines")
+            nc.vector.scalar_tensor_tensor(
+                out=live["cosines", c][:, pair, :].rearrange("p (k s) -> p k s", s=2),
+                in0=bank[:].rearrange("p (s k) -> p k s", s=2),
+                scalar=-1.0,
+                in1=live["p_factor", unit][:].rearrange("p (k s) -> p k s", s=2),
+                op0=ALU.mult,
+                op1=ALU.mult,
+            )
+
+        def finish(c, lo, hi):
+            dist = results.tile([P, K_CHUNK * S], F32, name="dist")
+            nc.vector.tensor_tensor(
+                out=dist[:, 0 : (hi - lo) * S].rearrange("p (k a s) -> p k a s", a=PAIRS, s=2),
+                in0=live["cosines", c][:].rearrange("p a (k s) -> p k a s", s=2)[:, lo:hi, :, :],
+                in1=q_factor[c][:, lo:hi].unsqueeze(2).unsqueeze(3).to_broadcast([P, hi - lo, PAIRS, 2]),
+                op=ALU.mult,
+            )
+            nc.sync.dma_start(
+                out=out_rows[:, (c * K_CHUNK + lo) * S : (c * K_CHUNK + hi) * S], in_=dist[:, 0 : (hi - lo) * S]
+            )
+
+        w_flip(0)
+        p_flip(0)
+        q_flip()
+        w_square(0, 0)
+        w_square(0, 1)
+        p_copy(0)
+        square_words(qq_values[:], live["q"])
+        copy_words(q_flipped[:].rearrange("p g n -> p (g n)"), live["q"])
+        w_quantise(0)
+        for pair in range(PAIRS):
+            if pair > 0:
+                p_copy(pair)
+            if pair + 1 < PAIRS:
+                p_flip(pair + 1)
+            p_square(pair)
+            if pair == 0:
+                quantise(qq_codes, qq_scales, qq_values[:])
+            p_times_q(pair)
+        q_norm(0)
+        w_flip(1)
+        w_square(1, 0)
+        w_square(1, 1)
+        w_quantise(1)
+
+        if NORMS_AHEAD:
+            p_norms(0)
+        for unit in range(UNITS):
+            c, pair = divmod(unit, PAIRS)
+            prepare = c + AHEAD < CHUNKS
+            if pair == 0:
+                if prepare:
+                    w_flip(c + AHEAD)
+                    w_square(c + AHEAD, 0)
+                if c > 0:
+                    q_norm(c)
+            if pair == 1 and prepare:
+                w_square(c + AHEAD, 1)
+            if not NORMS_AHEAD:
+                p_norms(unit)
+            elif unit + 1 < UNITS:
+                p_norms(unit + 1)
+            dots(unit)
+            if pair == 1 and prepare:
+                w_quantise(c + AHEAD)
+            if pair == PAIRS - 1:
+                if c + 1 < CHUNKS:
+                    finish(c, 0, K_CHUNK)
+                else:
+                    finish(c, 0, K_CHUNK // 2)
+                    finish(c, K_CHUNK // 2, K_CHUNK)

@@ -20,7 +20,6 @@ PAIRS = S // 2
 UNITS = CHUNKS * PAIRS
 AHEAD = 2
 SQUARE_ON_SCALAR = (False, True, True, False)
-NORMS_AHEAD = False
 
 FLOPS = 2 * (2 * B * S + B) * K * D
 
@@ -174,10 +173,10 @@ def tile_mpl_kernel(tc, p, q, W, out):
         def w_quantise(c):
             quantise(w2_codes[c], w2_scales[c], live["w2", c][:].rearrange("p g n -> p (g n)"))
 
-        def contract(sums, codes, scales, first, step, c):
+        def contract(sums, codes, scales, first, step, c, lo=0, width=K_CHUNK):
             for g in range(PASSES):
                 cols = slice((first + step * g) * P, (first + step * g + 1) * P)
-                k_cols = slice(g * K_CHUNK, (g + 1) * K_CHUNK)
+                k_cols = slice(g * K_CHUNK + lo, g * K_CHUNK + lo + width)
                 nc.tensor.matmul_mx(
                     out=sums,
                     lhsT=codes[:, cols].bitcast(FP8X4),
@@ -236,6 +235,36 @@ def tile_mpl_kernel(tc, p, q, W, out):
                 out=out_rows[:, (c * K_CHUNK + lo) * S : (c * K_CHUNK + hi) * S], in_=dist[:, 0 : (hi - lo) * S]
             )
 
+        def half_dots(c, pair, lo):
+            bank = banks.tile([P, 512], F32, name="bank")
+            for s in range(2):
+                contract(bank[:, s * P : (s + 1) * P], pq_codes[pair], pq_scales[pair], s, 2, c, lo, P)
+            cols = slice(2 * lo, 2 * (lo + P))
+            nc.vector.scalar_tensor_tensor(
+                out=live["cosines", c][:, pair, cols].rearrange("p (k s) -> p k s", s=2),
+                in0=bank[:, 0 : 2 * P].rearrange("p (s k) -> p k s", s=2),
+                scalar=-1.0,
+                in1=live["p_factor", c * PAIRS + pair][:, cols].rearrange("p (k s) -> p k s", s=2),
+                op0=ALU.mult,
+                op1=ALU.mult,
+            )
+
+        def finish_half(c, h, lo, hi):
+            if ("dist", c) not in live:
+                live["dist", c] = results.tile([P, K_CHUNK * S], F32, name="dist")
+            nc.vector.tensor_tensor(
+                out=live["dist", c][:].rearrange("p (k h a s) -> p k h a s", h=2, a=2, s=2)[:, lo:hi, h, :, :],
+                in0=live["cosines", c][:, 2 * h : 2 * h + 2, :].rearrange("p a (k s) -> p k a s", s=2)[:, lo:hi, :, :],
+                in1=q_factor[c][:, lo:hi].unsqueeze(2).unsqueeze(3).to_broadcast([P, hi - lo, 2, 2]),
+                op=ALU.mult,
+            )
+
+        def store_half(c, lo, hi):
+            nc.sync.dma_start(
+                out=out_rows[:, (c * K_CHUNK + lo) * S : (c * K_CHUNK + hi) * S],
+                in_=live["dist", c][:, lo * S : hi * S],
+            )
+
         w_flip(0)
         p_flip(0)
         q_flip()
@@ -260,9 +289,7 @@ def tile_mpl_kernel(tc, p, q, W, out):
         w_square(1, 1)
         w_quantise(1)
 
-        if NORMS_AHEAD:
-            p_norms(0)
-        for unit in range(UNITS):
+        for unit in range(UNITS - 1):
             c, pair = divmod(unit, PAIRS)
             prepare = c + AHEAD < CHUNKS
             if pair == 0:
@@ -273,16 +300,16 @@ def tile_mpl_kernel(tc, p, q, W, out):
                     q_norm(c)
             if pair == 1 and prepare:
                 w_square(c + AHEAD, 1)
-            if not NORMS_AHEAD:
-                p_norms(unit)
-            elif unit + 1 < UNITS:
-                p_norms(unit + 1)
+            p_norms(unit)
             dots(unit)
             if pair == 1 and prepare:
                 w_quantise(c + AHEAD)
             if pair == PAIRS - 1:
-                if c + 1 < CHUNKS:
-                    finish(c, 0, K_CHUNK)
-                else:
-                    finish(c, 0, K_CHUNK // 2)
-                    finish(c, K_CHUNK // 2, K_CHUNK)
+                finish(c, 0, K_CHUNK)
+        c = CHUNKS - 1
+        p_norms(UNITS - 1)
+        finish_half(c, 0, 0, K_CHUNK)
+        for lo in (0, P):
+            half_dots(c, PAIRS - 1, lo)
+            finish_half(c, 1, lo, lo + P)
+            store_half(c, lo, lo + P)

@@ -33,6 +33,7 @@ def tile_mpl_kernel(tc, p, q, W, out):
         staging = ctx.enter_context(tc.tile_pool(name="staging", bufs=2))
         results = ctx.enter_context(tc.tile_pool(name="results", bufs=3))
         banks = ctx.enter_context(tc.psum_pool(name="banks", bufs=8))
+        ctx.enter_context(tc.manual_schedule(engines={mybir.EngineType.DVE, mybir.EngineType.PE}))
 
         q_rows = inputs.tile([P, D], BF16, name="q_rows")
         p_rows = [inputs.tile([P, 2, D], BF16, name="p_rows%d" % pair) for pair in range(PAIRS)]
@@ -131,28 +132,35 @@ def tile_mpl_kernel(tc, p, q, W, out):
             else:
                 flat = live["p_flipped", pair][:].rearrange("p g n -> p (g n)")
                 nc.vector.tensor_tensor(out=values[:], in0=flat, in1=flat, op=ALU.mult)
-            quantise(pp_codes[pair], pp_scales[pair], values[:])
+            live["pp_values", pair] = values
 
-        def p_times_q(pair):
-            values = staging.tile([P, PASSES, 1024], BF16, name="pq_values", align_bytes=64)
-            for g in range(PASSES):
-                if SQUARE_ON_SCALAR[pair]:
-                    nc.vector.tensor_tensor(
-                        out=values[:, g, :].rearrange("p (s n u e) -> p s n u e", s=2, u=2, e=2),
-                        in0=live["p", pair, g][:].bitcast(BF16).rearrange("p (u s n e) -> p s n u e", u=2, s=2, e=2),
-                        in1=q_flipped[:, g, :]
-                        .rearrange("p (n u e) -> p n u e", u=2, e=2)
-                        .unsqueeze(1)
-                        .to_broadcast([P, 2, P, 2, 2]),
-                        op=ALU.mult,
-                    )
-                else:
-                    nc.vector.tensor_tensor(
-                        out=values[:, g, :].rearrange("p (s n) -> p s n", s=2),
-                        in0=live["p_flipped", pair][:, g, :].rearrange("p (s n) -> p s n", s=2),
-                        in1=q_flipped[:, g, :].unsqueeze(1).to_broadcast([P, 2, 4 * P]),
-                        op=ALU.mult,
-                    )
+        def pp_quantise(pair):
+            quantise(pp_codes[pair], pp_scales[pair], live["pp_values", pair][:])
+
+        def p_times_q(pair, g):
+            if g == 0:
+                live["pq_values", pair] = staging.tile([P, PASSES, 1024], BF16, name="pq_values", align_bytes=64)
+            values = live["pq_values", pair]
+            if SQUARE_ON_SCALAR[pair]:
+                nc.vector.tensor_tensor(
+                    out=values[:, g, :].rearrange("p (s n u e) -> p s n u e", s=2, u=2, e=2),
+                    in0=live["p", pair, g][:].bitcast(BF16).rearrange("p (u s n e) -> p s n u e", u=2, s=2, e=2),
+                    in1=q_flipped[:, g, :]
+                    .rearrange("p (n u e) -> p n u e", u=2, e=2)
+                    .unsqueeze(1)
+                    .to_broadcast([P, 2, P, 2, 2]),
+                    op=ALU.mult,
+                )
+            else:
+                nc.vector.tensor_tensor(
+                    out=values[:, g, :].rearrange("p (s n) -> p s n", s=2),
+                    in0=live["p_flipped", pair][:, g, :].rearrange("p (s n) -> p s n", s=2),
+                    in1=q_flipped[:, g, :].unsqueeze(1).to_broadcast([P, 2, 4 * P]),
+                    op=ALU.mult,
+                )
+
+        def pq_quantise(pair):
+            values = live["pq_values", pair]
             quantise(pq_codes[pair], pq_scales[pair], values[:].rearrange("p g n -> p (g n)"))
 
         def w_flip(c):
@@ -280,13 +288,21 @@ def tile_mpl_kernel(tc, p, q, W, out):
             if pair + 1 < PAIRS:
                 p_flip(pair + 1)
             p_square(pair)
+            p_times_q(pair, 0)
+            if pair > 0:
+                pq_quantise(pair - 1)
+            if not SQUARE_ON_SCALAR[pair]:
+                pp_quantise(pair)
+            p_times_q(pair, 1)
             if pair == 0:
                 quantise(qq_codes, qq_scales, qq_values[:])
-            p_times_q(pair)
+            if SQUARE_ON_SCALAR[pair]:
+                pp_quantise(pair)
         q_norm(0)
         w_flip(1)
         w_square(1, 0)
         w_square(1, 1)
+        pq_quantise(PAIRS - 1)
         w_quantise(1)
 
         for unit in range(UNITS - 1):
@@ -302,9 +318,9 @@ def tile_mpl_kernel(tc, p, q, W, out):
                 w_square(c + AHEAD, 1)
             p_norms(unit)
             dots(unit)
-            if pair == 1 and prepare:
-                w_quantise(c + AHEAD)
             if pair == PAIRS - 1:
+                if prepare:
+                    w_quantise(c + AHEAD)
                 finish(c, 0, K_CHUNK)
         c = CHUNKS - 1
         p_norms(UNITS - 1)

@@ -18,6 +18,8 @@ K_CHUNK = 256
 CHUNKS = K // K_CHUNK
 PAIRS = S // 2
 UNITS = CHUNKS * PAIRS
+GPSIMD_CHUNKS = (5, 5)
+K_PIECE = 64
 AHEAD = 2
 SQUARE_ON_SCALAR = (False, True, True, False)
 
@@ -33,7 +35,7 @@ def tile_mpl_kernel(tc, p, q, W, out):
         staging = ctx.enter_context(tc.tile_pool(name="staging", bufs=2))
         results = ctx.enter_context(tc.tile_pool(name="results", bufs=3))
         banks = ctx.enter_context(tc.psum_pool(name="banks", bufs=8))
-        ctx.enter_context(tc.manual_schedule(engines={mybir.EngineType.DVE, mybir.EngineType.PE}))
+        ctx.enter_context(tc.manual_schedule())
 
         q_rows = inputs.tile([P, D], BF16, name="q_rows")
         p_rows = [inputs.tile([P, 2, D], BF16, name="p_rows%d" % pair) for pair in range(PAIRS)]
@@ -233,12 +235,15 @@ def tile_mpl_kernel(tc, p, q, W, out):
 
         def finish(c, lo, hi):
             dist = results.tile([P, K_CHUNK * S], F32, name="dist")
-            nc.vector.tensor_tensor(
-                out=dist[:, 0 : (hi - lo) * S].rearrange("p (k a s) -> p k a s", a=PAIRS, s=2),
-                in0=live["cosines", c][:].rearrange("p a (k s) -> p k a s", s=2)[:, lo:hi, :, :],
-                in1=q_factor[c][:, lo:hi].unsqueeze(2).unsqueeze(3).to_broadcast([P, hi - lo, PAIRS, 2]),
-                op=ALU.mult,
-            )
+            on_gpsimd = c in GPSIMD_CHUNKS
+            step = P if on_gpsimd else hi - lo
+            for k0 in range(lo, hi, step):
+                (nc.gpsimd if on_gpsimd and k0 else nc.vector).tensor_tensor(
+                    out=dist[:, (k0 - lo) * S : (k0 - lo + step) * S].rearrange("p (k a s) -> p k a s", a=PAIRS, s=2),
+                    in0=live["cosines", c][:].rearrange("p a (k s) -> p k a s", s=2)[:, k0 : k0 + step, :, :],
+                    in1=q_factor[c][:, k0 : k0 + step].unsqueeze(2).unsqueeze(3).to_broadcast([P, step, PAIRS, 2]),
+                    op=ALU.mult,
+                )
             nc.sync.dma_start(
                 out=out_rows[:, (c * K_CHUNK + lo) * S : (c * K_CHUNK + hi) * S], in_=dist[:, 0 : (hi - lo) * S]
             )
@@ -257,10 +262,10 @@ def tile_mpl_kernel(tc, p, q, W, out):
                 op1=ALU.mult,
             )
 
-        def finish_half(c, h, lo, hi):
+        def finish_half(c, h, lo, hi, engine):
             if ("dist", c) not in live:
                 live["dist", c] = results.tile([P, K_CHUNK * S], F32, name="dist")
-            nc.vector.tensor_tensor(
+            engine.tensor_tensor(
                 out=live["dist", c][:].rearrange("p (k h a s) -> p k h a s", h=2, a=2, s=2)[:, lo:hi, h, :, :],
                 in0=live["cosines", c][:, 2 * h : 2 * h + 2, :].rearrange("p a (k s) -> p k a s", s=2)[:, lo:hi, :, :],
                 in1=q_factor[c][:, lo:hi].unsqueeze(2).unsqueeze(3).to_broadcast([P, hi - lo, 2, 2]),
@@ -279,8 +284,8 @@ def tile_mpl_kernel(tc, p, q, W, out):
         w_square(0, 0)
         w_square(0, 1)
         p_copy(0)
-        square_words(qq_values[:], live["q"])
         copy_words(q_flipped[:].rearrange("p g n -> p (g n)"), live["q"])
+        square_words(qq_values[:], live["q"])
         w_quantise(0)
         for pair in range(PAIRS):
             if pair > 0:
@@ -298,7 +303,6 @@ def tile_mpl_kernel(tc, p, q, W, out):
                 quantise(qq_codes, qq_scales, qq_values[:])
             if SQUARE_ON_SCALAR[pair]:
                 pp_quantise(pair)
-        q_norm(0)
         w_flip(1)
         w_square(1, 0)
         w_square(1, 1)
@@ -312,20 +316,28 @@ def tile_mpl_kernel(tc, p, q, W, out):
                 if prepare:
                     w_flip(c + AHEAD)
                     w_square(c + AHEAD, 0)
-                if c > 0:
-                    q_norm(c)
-            if pair == 1 and prepare:
-                w_square(c + AHEAD, 1)
+            if pair == 1:
+                q_norm(c)
+                if prepare:
+                    w_square(c + AHEAD, 1)
             p_norms(unit)
             dots(unit)
             if pair == PAIRS - 1:
                 if prepare:
                     w_quantise(c + AHEAD)
-                finish(c, 0, K_CHUNK)
+                if c < CHUNKS - 2:
+                    finish(c, 0, K_CHUNK)
+            if c == CHUNKS - 2 and pair == 2:
+                finish_half(c, 0, 0, K_CHUNK, nc.vector)
+            if c == CHUNKS - 2 and pair == 3:
+                for lo in (0, P):
+                    finish_half(c, 1, lo, lo + P, nc.gpsimd)
+                    store_half(c, lo, lo + P)
         c = CHUNKS - 1
         p_norms(UNITS - 1)
-        finish_half(c, 0, 0, K_CHUNK)
+        finish_half(c, 0, 0, K_CHUNK, nc.vector)
         for lo in (0, P):
             half_dots(c, PAIRS - 1, lo)
-            finish_half(c, 1, lo, lo + P)
+        for lo in (0, P):
+            finish_half(c, 1, lo, lo + P, nc.vector)
             store_half(c, lo, lo + P)

@@ -18,7 +18,7 @@ K_CHUNK = 256
 CHUNKS = K // K_CHUNK
 PAIRS = S // 2
 UNITS = CHUNKS * PAIRS
-GPSIMD_CHUNKS = (5, 5)
+GPSIMD_CHUNKS = (1, 2, 3, 4, 5)
 K_PIECE = 64
 AHEAD = 2
 SQUARE_ON_SCALAR = (False, True, True, False)
@@ -48,8 +48,10 @@ def tile_mpl_kernel(tc, p, q, W, out):
             rows = W[K_CHUNK * c : K_CHUNK * (c + 1), :]
             nc.sync.dma_start(out=w_rows[c][:], in_=rows.rearrange("(t r) d -> r t d", r=P))
 
-        load_w(0)
-        load_p(0)
+        for t in range(2):
+            nc.sync.dma_start(out=w_rows[0][:, t, :], in_=W[P * t : P * (t + 1), :])
+        for t in range(2):
+            nc.sync.dma_start(out=p_rows[0][:, t, :], in_=p[:, t, :])
         nc.sync.dma_start(out=q_rows[:], in_=q[:, S - 1, :])
         for pair in range(1, PAIRS):
             load_p(pair)
@@ -76,13 +78,24 @@ def tile_mpl_kernel(tc, p, q, W, out):
         q_factor = [operands.tile([P, K_CHUNK], F32, name="q_factor%d" % c) for c in range(CHUNKS)]
         live = {}
 
-        def flip(rows, g):
+        def w_sort(c):
+            sorted_rows = staging.tile([P, 2, D], BF16, name="w_sorted")
+            live["sorted", c] = sorted_rows
+            nc.vector.tensor_copy(
+                out=sorted_rows[:].rearrange("p t n -> p (t n)").bitcast(F32).rearrange("p (x u r) -> p x u r", u=2, r=P),
+                in_=w_rows[c][:].rearrange("p t n -> p (t n)").bitcast(F32).rearrange("p (x r u) -> p x u r", u=2, r=P),
+            )
+
+        def flip(rows, g, is_sorted=False):
             bank = banks.tile([P, 512], F32, name="bank")
-            for u in range(2):
-                for t in range(2):
+            for t in range(2):
+                for u in range(2):
+                    words = rows[:, t, :].bitcast(F32)
                     nc.tensor.transpose(
                         out=bank[:, u * 256 + t * P : u * 256 + (t + 1) * P],
-                        in_=rows[:, t, :].bitcast(F32)[:, 256 * g + u : 256 * (g + 1) : 2],
+                        in_=words[:, 256 * g + P * u : 256 * g + P * (u + 1)]
+                        if is_sorted
+                        else words[:, 256 * g + u : 256 * (g + 1) : 2],
                         identity=identity[:],
                     )
             return bank
@@ -167,7 +180,7 @@ def tile_mpl_kernel(tc, p, q, W, out):
 
         def w_flip(c):
             for g in range(PASSES):
-                live["w", c, g] = flip(w_rows[c], g)
+                live["w", c, g] = flip(live["sorted", c], g, True) if ("sorted", c) in live else flip(w_rows[c], g)
 
         def w_square(c, g):
             if g == 0:
@@ -327,6 +340,8 @@ def tile_mpl_kernel(tc, p, q, W, out):
                     w_quantise(c + AHEAD)
                 if c < CHUNKS - 2:
                     finish(c, 0, K_CHUNK)
+                if c + AHEAD + 2 < CHUNKS:
+                    w_sort(c + AHEAD + 2)
             if c == CHUNKS - 2 and pair == 2:
                 finish_half(c, 0, 0, K_CHUNK, nc.vector)
             if c == CHUNKS - 2 and pair == 3:
@@ -335,9 +350,12 @@ def tile_mpl_kernel(tc, p, q, W, out):
                     store_half(c, lo, lo + P)
         c = CHUNKS - 1
         p_norms(UNITS - 1)
-        finish_half(c, 0, 0, K_CHUNK, nc.vector)
-        for lo in (0, P):
-            half_dots(c, PAIRS - 1, lo)
-        for lo in (0, P):
-            finish_half(c, 1, lo, lo + P, nc.vector)
-            store_half(c, lo, lo + P)
+        half_dots(c, PAIRS - 1, 0)
+        finish_half(c, 0, 0, P, nc.vector)
+        finish_half(c, 1, 0, P, nc.vector)
+        store_half(c, 0, P)
+        half_dots(c, PAIRS - 1, P)
+        finish_half(c, 0, P, K_CHUNK, nc.vector)
+        for lo in (P, P + 64):
+            finish_half(c, 1, lo, lo + 64, nc.vector)
+            store_half(c, lo, lo + 64)

@@ -48,8 +48,10 @@ def tile_mpl_kernel(tc, p, q, W, out):
             rows = W[K_CHUNK * c : K_CHUNK * (c + 1), :]
             nc.sync.dma_start(out=w_rows[c][:], in_=rows.rearrange("(t r) d -> r t d", r=P))
 
-        for t in range(2):
-            nc.sync.dma_start(out=w_rows[0][:, t, :], in_=W[P * t : P * (t + 1), :])
+        for g in range(PASSES):
+            for t in range(2):
+                cols = slice(512 * g, 512 * (g + 1))
+                nc.sync.dma_start(out=w_rows[0][:, t, cols], in_=W[P * t : P * (t + 1), cols])
         for t in range(2):
             nc.sync.dma_start(out=p_rows[0][:, t, :], in_=p[:, t, :])
         nc.sync.dma_start(out=q_rows[:], in_=q[:, S - 1, :])
@@ -174,6 +176,16 @@ def tile_mpl_kernel(tc, p, q, W, out):
                     op=ALU.mult,
                 )
 
+        def p_times_q_copied(pair):
+            values = staging.tile([P, PASSES, 1024], BF16, name="pq_values", align_bytes=64)
+            live["pq_values", pair] = values
+            nc.vector.tensor_tensor(
+                out=values[:].rearrange("p g (s n) -> p g s n", s=2),
+                in0=live["p_flipped", pair][:].rearrange("p g (s n) -> p g s n", s=2),
+                in1=q_flipped[:].unsqueeze(2).to_broadcast([P, PASSES, 2, 4 * P]),
+                op=ALU.mult,
+            )
+
         def pq_quantise(pair):
             values = live["pq_values", pair]
             quantise(pq_codes[pair], pq_scales[pair], values[:].rearrange("p g n -> p (g n)"))
@@ -249,9 +261,11 @@ def tile_mpl_kernel(tc, p, q, W, out):
         def finish(c, lo, hi):
             dist = results.tile([P, K_CHUNK * S], F32, name="dist")
             on_gpsimd = c in GPSIMD_CHUNKS
-            step = P if on_gpsimd else hi - lo
-            for k0 in range(lo, hi, step):
-                (nc.gpsimd if on_gpsimd and k0 else nc.vector).tensor_tensor(
+            cut = 160 if on_gpsimd else hi
+            for k0, step in ((lo, cut - lo), (cut, hi - cut)):
+                if step == 0:
+                    continue
+                (nc.gpsimd if k0 else nc.vector).tensor_tensor(
                     out=dist[:, (k0 - lo) * S : (k0 - lo + step) * S].rearrange("p (k a s) -> p k a s", a=PAIRS, s=2),
                     in0=live["cosines", c][:].rearrange("p a (k s) -> p k a s", s=2)[:, k0 : k0 + step, :, :],
                     in1=q_factor[c][:, k0 : k0 + step].unsqueeze(2).unsqueeze(3).to_broadcast([P, step, PAIRS, 2]),
@@ -306,12 +320,16 @@ def tile_mpl_kernel(tc, p, q, W, out):
             if pair + 1 < PAIRS:
                 p_flip(pair + 1)
             p_square(pair)
-            p_times_q(pair, 0)
+            if SQUARE_ON_SCALAR[pair]:
+                p_times_q(pair, 0)
+            else:
+                p_times_q_copied(pair)
             if pair > 0:
                 pq_quantise(pair - 1)
-            if not SQUARE_ON_SCALAR[pair]:
+            if SQUARE_ON_SCALAR[pair]:
+                p_times_q(pair, 1)
+            else:
                 pp_quantise(pair)
-            p_times_q(pair, 1)
             if pair == 0:
                 quantise(qq_codes, qq_scales, qq_values[:])
             if SQUARE_ON_SCALAR[pair]:

from contextlib import ExitStack

import concourse.mybir as mybir
from concourse.masks import make_identity

F32 = mybir.dt.float32
BF16 = mybir.dt.bfloat16
U32 = mybir.dt.uint32
U8 = mybir.dt.uint8
FP8X4 = mybir.dt.float8_e4m3fn_x4
ACT = mybir.ActivationFunctionType
ALU = mybir.AluOpType

P = 128
B, S, D, K = 128, 8, 1024, 2048
PASSES = D // (4 * P)
K_CHUNK = 256
CHUNKS = K // K_CHUNK
PAIRS = S // 2
UNITS = CHUNKS * PAIRS
GPSIMD_CHUNKS = (1, 2, 3, 4, 5)
K_PIECE = 64
AHEAD = 2
SQUARE_ON_SCALAR = (False, True, True, False)

FLOPS = 2 * (2 * B * S + B) * K * D


def tile_mpl_kernel(tc, p, q, W, out):
    nc = tc.nc
    out_rows = out.rearrange("b s k -> b (s k)")
    with ExitStack() as ctx:
        inputs = ctx.enter_context(tc.tile_pool(name="inputs", bufs=1))
        operands = ctx.enter_context(tc.tile_pool(name="operands", bufs=1))
        staging = ctx.enter_context(tc.tile_pool(name="staging", bufs=2))
        results = ctx.enter_context(tc.tile_pool(name="results", bufs=3))
        banks = ctx.enter_context(tc.psum_pool(name="banks", bufs=8))
        ctx.enter_context(tc.manual_schedule())

        q_rows = inputs.tile([P, D], BF16, name="q_rows")
        p_rows = [inputs.tile([P, 2, D], BF16, name="p_rows%d" % pair) for pair in range(PAIRS)]
        w_rows = [inputs.tile([P, 2, D], BF16, name="w_rows%d" % c) for c in range(CHUNKS)]

        def load_p(pair):
            nc.sync.dma_start(out=p_rows[pair][:], in_=p[:, 2 * pair : 2 * pair + 2, :])

        def load_w(c):
            rows = W[K_CHUNK * c : K_CHUNK * (c + 1), :]
            nc.sync.dma_start(out=w_rows[c][:], in_=rows.rearrange("(t r) d -> r t d", r=P))

        for g in range(PASSES):
            for t in range(2):
                cols = slice(512 * g, 512 * (g + 1))
                nc.sync.dma_start(out=w_rows[0][:, t, cols], in_=W[P * t : P * (t + 1), cols])
        for t in range(2):
            nc.sync.dma_start(out=p_rows[0][:, t, :], in_=p[:, t, :])
        nc.sync.dma_start(out=q_rows[:], in_=q[:, S - 1, :])
        for pair in range(1, PAIRS):
            load_p(pair)
        for c in range(1, CHUNKS):
            load_w(c)

        identity = inputs.tile([P, P], F32, name="identity")
        make_identity(nc, identity[:])
        one = inputs.tile([P, 1], F32, name="one")
        nc.vector.memset(one[:], 1.0)
        warm = inputs.tile([P, 1], F32, name="warm")
        nc.scalar.activation(out=warm[:], in_=one[:], func=ACT.Abs_reciprocal_sqrt)

        q_flipped = inputs.tile([P, PASSES, 4 * P], BF16, name="q_flipped")
        qq_values = inputs.tile([P, PASSES * 4 * P], BF16, name="qq_values", align_bytes=64)
        qq_codes = operands.tile([P, PASSES * P], U32, name="qq_codes", align_bytes=64)
        qq_scales = operands.tile([P, PASSES * P], U8, name="qq_scales", align_bytes=64)
        pq_codes = [operands.tile([P, 512], U32, name="pq_codes%d" % i, align_bytes=64) for i in range(PAIRS)]
        pq_scales = [operands.tile([P, 512], U8, name="pq_scales%d" % i, align_bytes=64) for i in range(PAIRS)]
        pp_codes = [operands.tile([P, 512], U32, name="pp_codes%d" % i, align_bytes=64) for i in range(PAIRS)]
        pp_scales = [operands.tile([P, 512], U8, name="pp_scales%d" % i, align_bytes=64) for i in range(PAIRS)]
        w2_codes = [operands.tile([P, 512], U32, name="w2_codes%d" % c, align_bytes=64) for c in range(CHUNKS)]
        w2_scales = [operands.tile([P, 512], U8, name="w2_scales%d" % c, align_bytes=64) for c in range(CHUNKS)]
        q_factor = [operands.tile([P, K_CHUNK], F32, name="q_factor%d" % c) for c in range(CHUNKS)]
        live = {}

        def w_sort(c):
            sorted_rows = staging.tile([P, 2, D], BF16, name="w_sorted")
            live["sorted", c] = sorted_rows
            nc.vector.tensor_copy(
                out=sorted_rows[:].rearrange("p t n -> p (t n)").bitcast(F32).rearrange("p (x u r) -> p x u r", u=2, r=P),
                in_=w_rows[c][:].rearrange("p t n -> p (t n)").bitcast(F32).rearrange("p (x r u) -> p x u r", u=2, r=P),
            )

        def flip(rows, g, is_sorted=False):
            bank = banks.tile([P, 512], F32, name="bank")
            for t in range(2):
                for u in range(2):
                    words = rows[:, t, :].bitcast(F32)
                    nc.tensor.transpose(
                        out=bank[:, u * 256 + t * P : u * 256 + (t + 1) * P],
                        in_=words[:, 256 * g + P * u : 256 * g + P * (u + 1)]
                        if is_sorted
                        else words[:, 256 * g + u : 256 * (g + 1) : 2],
                        identity=identity[:],
                    )
            return bank

        def copy_words(dst, bank):
            nc.scalar.copy(
                out=dst.bitcast(F32).rearrange("p (n u) -> p n u", u=2),
                in_=bank[:].rearrange("p (u n) -> p n u", u=2),
            )

        def square_words(dst, bank):
            nc.scalar.activation(
                out=dst.rearrange("p (n u e) -> p n u e", u=2, e=2),
                in_=bank[:].bitcast(BF16).rearrange("p (u n e) -> p n u e", u=2, e=2),
                func=ACT.Square,
            )

        def quantise(codes, scales, values):
            nc.vector.quantize_mx(out=codes[:].bitcast(FP8X4), scales=scales[:], in_=values)

        def q_flip():
            bank = banks.tile([P, 512], F32, name="bank")
            for u in range(2):
                for g in range(PASSES):
                    nc.tensor.transpose(
                        out=bank[:, u * 256 + g * P : u * 256 + (g + 1) * P],
                        in_=q_rows[:].bitcast(F32)[:, 256 * g + u : 256 * (g + 1) : 2],
                        identity=identity[:],
                    )
            live["q"] = bank

        def p_flip(pair):
            for g in range(PASSES):
                live["p", pair, g] = flip(p_rows[pair], g)

        def p_copy(pair):
            if SQUARE_ON_SCALAR[pair]:
                return
            flipped = staging.tile([P, PASSES, 1024], BF16, name="p_flipped")
            live["p_flipped", pair] = flipped
            for g in range(PASSES):
                copy_words(flipped[:, g, :], live["p", pair, g])

        def p_square(pair):
            values = staging.tile([P, PASSES * 1024], BF16, name="pp_values", align_bytes=64)
            if SQUARE_ON_SCALAR[pair]:
                for g in range(PASSES):
                    square_words(values[:, g * 1024 : (g + 1) * 1024], live["p", pair, g])
            else:
                flat = live["p_flipped", pair][:].rearrange("p g n -> p (g n)")
                nc.vector.tensor_tensor(out=values[:], in0=flat, in1=flat, op=ALU.mult)
            live["pp_values", pair] = values

        def pp_quantise(pair):
            quantise(pp_codes[pair], pp_scales[pair], live["pp_values", pair][:])

        def p_times_q(pair, g):
            if g == 0:
                live["pq_values", pair] = staging.tile([P, PASSES, 1024], BF16, name="pq_values", align_bytes=64)
            values = live["pq_values", pair]
            if SQUARE_ON_SCALAR[pair]:
                nc.vector.tensor_tensor(
                    out=values[:, g, :].rearrange("p (s n u e) -> p s n u e", s=2, u=2, e=2),
                    in0=live["p", pair, g][:].bitcast(BF16).rearrange("p (u s n e) -> p s n u e", u=2, s=2, e=2),
                    in1=q_flipped[:, g, :]
                    .rearrange("p (n u e) -> p n u e", u=2, e=2)
                    .unsqueeze(1)
                    .to_broadcast([P, 2, P, 2, 2]),
                    op=ALU.mult,
                )
            else:
                nc.vector.tensor_tensor(
                    out=values[:, g, :].rearrange("p (s n) -> p s n", s=2),
                    in0=live["p_flipped", pair][:, g, :].rearrange("p (s n) -> p s n", s=2),
                    in1=q_flipped[:, g, :].unsqueeze(1).to_broadcast([P, 2, 4 * P]),
                    op=ALU.mult,
                )

        def p_times_q_copied(pair):
            values = staging.tile([P, PASSES, 1024], BF16, name="pq_values", align_bytes=64)
            live["pq_values", pair] = values
            nc.vector.tensor_tensor(
                out=values[:].rearrange("p g (s n) -> p g s n", s=2),
                in0=live["p_flipped", pair][:].rearrange("p g (s n) -> p g s n", s=2),
                in1=q_flipped[:].unsqueeze(2).to_broadcast([P, PASSES, 2, 4 * P]),
                op=ALU.mult,
            )

        def pq_quantise(pair):
            values = live["pq_values", pair]
            quantise(pq_codes[pair], pq_scales[pair], values[:].rearrange("p g n -> p (g n)"))

        def w_flip(c):
            for g in range(PASSES):
                live["w", c, g] = flip(live["sorted", c], g, True) if ("sorted", c) in live else flip(w_rows[c], g)

        def w_square(c, g):
            if g == 0:
                live["w2", c] = staging.tile([P, PASSES, 1024], BF16, name="w2_values", align_bytes=64)
            values = live["w2", c]
            if c == 0:
                flipped = staging.tile([P, 1024], BF16, name="w_flipped")
                copy_words(flipped[:], live["w", c, g])
                nc.vector.tensor_tensor(out=values[:, g, :], in0=flipped[:], in1=flipped[:], op=ALU.mult)
            else:
                square_words(values[:, g, :], live["w", c, g])

        def w_quantise(c):
            quantise(w2_codes[c], w2_scales[c], live["w2", c][:].rearrange("p g n -> p (g n)"))

        def contract(sums, codes, scales, first, step, c, lo=0, width=K_CHUNK):
            for g in range(PASSES):
                cols = slice((first + step * g) * P, (first + step * g + 1) * P)
                k_cols = slice(g * K_CHUNK + lo, g * K_CHUNK + lo + width)
                nc.tensor.matmul_mx(
                    out=sums,
                    lhsT=codes[:, cols].bitcast(FP8X4),
                    lhsT_scale=scales[:, cols],
                    rhs=w2_codes[c][:, k_cols].bitcast(FP8X4),
                    rhs_scale=w2_scales[c][:, k_cols],
                    start=(g == 0),
                    stop=(g == PASSES - 1),
                )

        def q_norm(c):
            bank = banks.tile([P, 512], F32, name="bank")
            contract(bank[:, 0:K_CHUNK], qq_codes, qq_scales, 0, 1, c)
            nc.scalar.activation(
                out=q_factor[c][:], in_=bank[:, 0:K_CHUNK], func=ACT.Abs_reciprocal_sqrt, scale=float(D * D)
            )

        def p_norms(unit):
            c, pair = divmod(unit, PAIRS)
            bank = banks.tile([P, 512], F32, name="bank")
            for s in range(2):
                contract(bank[:, s * K_CHUNK : (s + 1) * K_CHUNK], pp_codes[pair], pp_scales[pair], s, 2, c)
            factor = results.tile([P, 2 * K_CHUNK], F32, name="p_factor")
            live["p_factor", unit] = factor
            nc.scalar.activation(
                out=factor[:].rearrange("p (k s) -> p k s", s=2),
                in_=bank[:].rearrange("p (s k) -> p k s", s=2),
                func=ACT.Abs_reciprocal_sqrt,
            )

        def dots(unit):
            c, pair = divmod(unit, PAIRS)
            bank = banks.tile([P, 512], F32, name="bank")
            for s in range(2):
                contract(bank[:, s * K_CHUNK : (s + 1) * K_CHUNK], pq_codes[pair], pq_scales[pair], s, 2, c)
            if pair == 0:
                live["cosines", c] = results.tile([P, PAIRS, 2 * K_CHUNK], F32, name="cosines")
            nc.vector.scalar_tensor_tensor(
                out=live["cosines", c][:, pair, :].rearrange("p (k s) -> p k s", s=2),
                in0=bank[:].rearrange("p (s k) -> p k s", s=2),
                scalar=-1.0,
                in1=live["p_factor", unit][:].rearrange("p (k s) -> p k s", s=2),
                op0=ALU.mult,
                op1=ALU.mult,
            )

        def finish(c, lo, hi):
            dist = results.tile([P, K_CHUNK * S], F32, name="dist")
            on_gpsimd = c in GPSIMD_CHUNKS
            cut = 160 if on_gpsimd else hi
            for k0, step in ((lo, cut - lo), (cut, hi - cut)):
                if step == 0:
                    continue
                (nc.gpsimd if k0 else nc.vector).tensor_tensor(
                    out=dist[:, (k0 - lo) * S : (k0 - lo + step) * S].rearrange("p (k a s) -> p k a s", a=PAIRS, s=2),
                    in0=live["cosines", c][:].rearrange("p a (k s) -> p k a s", s=2)[:, k0 : k0 + step, :, :],
                    in1=q_factor[c][:, k0 : k0 + step].unsqueeze(2).unsqueeze(3).to_broadcast([P, step, PAIRS, 2]),
                    op=ALU.mult,
                )
            nc.sync.dma_start(
                out=out_rows[:, (c * K_CHUNK + lo) * S : (c * K_CHUNK + hi) * S], in_=dist[:, 0 : (hi - lo) * S]
            )

        def half_dots(c, pair, lo):
            bank = banks.tile([P, 512], F32, name="bank")
            for s in range(2):
                contract(bank[:, s * P : (s + 1) * P], pq_codes[pair], pq_scales[pair], s, 2, c, lo, P)
            cols = slice(2 * lo, 2 * (lo + P))
            nc.vector.scalar_tensor_tensor(
                out=live["cosines", c][:, pair, cols].rearrange("p (k s) -> p k s", s=2),
                in0=bank[:, 0 : 2 * P].rearrange("p (s k) -> p k s", s=2),
                scalar=-1.0,
                in1=live["p_factor", c * PAIRS + pair][:, cols].rearrange("p (k s) -> p k s", s=2),
                op0=ALU.mult,
                op1=ALU.mult,
            )

        def finish_half(c, h, lo, hi, engine):
            if ("dist", c) not in live:
                live["dist", c] = results.tile([P, K_CHUNK * S], F32, name="dist")
            engine.tensor_tensor(
                out=live["dist", c][:].rearrange("p (k h a s) -> p k h a s", h=2, a=2, s=2)[:, lo:hi, h, :, :],
                in0=live["cosines", c][:, 2 * h : 2 * h + 2, :].rearrange("p a (k s) -> p k a s", s=2)[:, lo:hi, :, :],
                in1=q_factor[c][:, lo:hi].unsqueeze(2).unsqueeze(3).to_broadcast([P, hi - lo, 2, 2]),
                op=ALU.mult,
            )

        def store_half(c, lo, hi):
            nc.sync.dma_start(
                out=out_rows[:, (c * K_CHUNK + lo) * S : (c * K_CHUNK + hi) * S],
                in_=live["dist", c][:, lo * S : hi * S],
            )

        w_flip(0)
        p_flip(0)
        q_flip()
        w_square(0, 0)
        w_square(0, 1)
        p_copy(0)
        copy_words(q_flipped[:].rearrange("p g n -> p (g n)"), live["q"])
        square_words(qq_values[:], live["q"])
        w_quantise(0)
        for pair in range(PAIRS):
            if pair > 0:
                p_copy(pair)
            if pair + 1 < PAIRS:
                p_flip(pair + 1)
            p_square(pair)
            if SQUARE_ON_SCALAR[pair]:
                p_times_q(pair, 0)
            else:
                p_times_q_copied(pair)
            if pair > 0:
                pq_quantise(pair - 1)
            if SQUARE_ON_SCALAR[pair]:
                p_times_q(pair, 1)
            else:
                pp_quantise(pair)
            if pair == 0:
                quantise(qq_codes, qq_scales, qq_values[:])
            if SQUARE_ON_SCALAR[pair]:
                pp_quantise(pair)
        w_flip(1)
        w_square(1, 0)
        w_square(1, 1)
        pq_quantise(PAIRS - 1)
        w_quantise(1)

        for unit in range(UNITS - 1):
            c, pair = divmod(unit, PAIRS)
            prepare = c + AHEAD < CHUNKS
            if pair == 0:
                if prepare:
                    w_flip(c + AHEAD)
                    w_square(c + AHEAD, 0)
            if pair == 1:
                q_norm(c)
                if prepare:
                    w_square(c + AHEAD, 1)
            p_norms(unit)
            dots(unit)
            if pair == PAIRS - 1:
                if prepare:
                    w_quantise(c + AHEAD)
                if c < CHUNKS - 2:
                    finish(c, 0, K_CHUNK)
                if c + AHEAD + 2 < CHUNKS:
                    w_sort(c + AHEAD + 2)
            if c == CHUNKS - 2 and pair == 2:
                finish_half(c, 0, 0, K_CHUNK, nc.vector)
            if c == CHUNKS - 2 and pair == 3:
                for lo in (0, P):
                    finish_half(c, 1, lo, lo + P, nc.gpsimd)
                    store_half(c, lo, lo + P)
        c = CHUNKS - 1
        p_norms(UNITS - 1)
        half_dots(c, PAIRS - 1, 0)
        finish_half(c, 0, 0, P, nc.vector)
        finish_half(c, 1, 0, P, nc.vector)
        store_half(c, 0, P)
        half_dots(c, PAIRS - 1, P)
        finish_half(c, 0, P, K_CHUNK, nc.vector)
        for lo in (P, P + 64):
            finish_half(c, 1, lo, lo + 64, nc.vector)
            store_half(c, lo, lo + 64)
